import numpy as np
import ml_dtypes


def mxq(x, axis, fmt="e4m3"):
    dtype, down = {"e4m3": (ml_dtypes.float8_e4m3fn, 7), "e5m2": (ml_dtypes.float8_e5m2, 14)}[fmt]
    v = np.moveaxis(np.asarray(x, np.float32).astype(ml_dtypes.bfloat16).astype(np.float64), axis, -1)
    blocks = v.reshape(v.shape[:-1] + (-1, 32))
    amax = np.abs(blocks).max(-1, keepdims=True)
    byte = np.maximum(np.where(amax > 0, np.frexp(amax)[1] - 1 + 127, 0) - down, 1)
    scale = np.exp2(byte - 127.0)
    codes = (blocks / scale).astype(np.float32).astype(dtype).astype(np.float64)
    return np.moveaxis((codes * scale).reshape(v.shape), -1, axis)


WIDE = False


def mx_kscale(k):
    if not WIDE:
        return np.ones(k)
    levels = np.array([10, -10, 5, -5, 0])
    if k % 512:
        return np.exp2(np.random.permutation(np.resize(levels, k // 32))).repeat(32)
    a = np.empty((k // 512, 16))
    for p in range(k // 512):
        a[p, :8] = np.random.permutation(np.resize(levels, 8))
        for g in range(8):
            far = levels[np.abs(levels - a[p, g]) >= 10]
            a[p, g + 8] = far[np.random.randint(len(far))]
    return np.exp2(a.ravel()).repeat(32)


BF16 = ml_dtypes.bfloat16


def bf(x):
    return np.asarray(x, np.float32).astype(BF16)


def f64(x):
    return np.asarray(x).astype(np.float64)


B, K, N = 1024, 2048, 2048
EPS = 1e-5
GELU_C = 0.7978845608


def setup_inputs():
    s = mx_kscale(K)
    return {"x": bf(np.random.standard_normal((B, K)) * s),
            "weight": bf(np.random.standard_normal((K, N)) * np.sqrt(2.0 / K) / s[:, None]),
            "bn_gamma": bf(np.random.uniform(0.5, 1.5, N)),
            "bn_beta": bf(np.random.standard_normal(N) * 0.1),
            "bn_mean": bf(np.random.standard_normal(N) * 0.1),
            "bn_var": bf(np.random.uniform(0.5, 1.5, N))}


def reference(x, weight, bn_gamma, bn_beta, bn_mean, bn_var):
    acc = mxq(f64(x), 1, "e4m3") @ mxq(f64(weight), 0, "e4m3")
    x_norm = (acc - f64(bn_mean)) / np.sqrt(f64(bn_var) + EPS)
    bn_out = f64(bn_gamma) * x_norm + f64(bn_beta)
    gelu = 0.5 * bn_out * (1.0 + np.tanh(GELU_C * (bn_out + 0.044715 * bn_out * bn_out * bn_out)))
    return np.maximum(gelu, 0.0)

@@ -1,0 +1,303 @@
+from contextlib import ExitStack
+
+import concourse.mybir as mybir
+from concourse.masks import make_identity
+
+FP8X4 = mybir.dt.float8_e4m3fn_x4
+BF16 = mybir.dt.bfloat16
+F32 = mybir.dt.float32
+U32 = mybir.dt.uint32
+U8 = mybir.dt.uint8
+ACT = mybir.ActivationFunctionType
+ALU = mybir.AluOpType
+
+B, K, N = 1024, 2048, 2048
+EPS = 1e-5
+FLOPS = 2 * B * K * N
+
+P = 128
+PACK = 4
+PASSES = K // (P * PACK)
+ROW_TILES = B // P
+PAIRS = ROW_TILES // 2
+HALF_TILES = 4
+HALF = HALF_TILES * P
+COL_TILES = 4
+BLOCK = COL_TILES * P
+N_BLOCKS = N // BLOCK
+UNITS = 2 * N_BLOCKS
+LAST = UNITS - 1
+SHARED_BLOCKS = 2
+VECTOR_COLS = BLOCK // 2
+
+
+def tile_modelnew_kernel(tc, x, weight, bn_gamma, bn_beta, bn_mean, bn_var, out):
+    nc = tc.nc
+    x_v = x.rearrange("(p t) k -> p t k", t=ROW_TILES)
+    out_v = out.rearrange("(p t) n -> p t n", t=ROW_TILES)
+
+    with ExitStack() as ctx:
+        const = ctx.enter_context(tc.tile_pool(name="const", bufs=1))
+        keep = ctx.enter_context(tc.tile_pool(name="keep", bufs=1))
+        wg_pool = ctx.enter_context(tc.tile_pool(name="wg_pool", bufs=3))
+        xg_pool = ctx.enter_context(tc.tile_pool(name="xg_pool", bufs=2 * PASSES))
+        g_pool = ctx.enter_context(tc.tile_pool(name="g_pool", bufs=2 * COL_TILES))
+        o_pool = ctx.enter_context(tc.tile_pool(name="o_pool", bufs=3))
+        ps_acc = ctx.enter_context(tc.psum_pool(name="ps_acc", bufs=4))
+        ps_tr = ctx.enter_context(tc.psum_pool(name="ps_tr", bufs=4))
+        ctx.enter_context(tc.manual_schedule())
+
+        x_raw = [keep.tile([P, 2, K], BF16, name="x_raw%d" % pair) for pair in range(PAIRS)]
+        w_raw = [keep.tile([P, PACK * PASSES, BLOCK], BF16, name="w_raw%d" % nb) for nb in range(N_BLOCKS)]
+        w_codes = keep.tile([P, PASSES, N], U32, name="w_codes", align_bytes=64)
+        w_scales = keep.tile([P, PASSES, N], U8, name="w_scales", align_bytes=64)
+        x_codes = keep.tile([P, PASSES, B], U32, name="x_codes", align_bytes=64)
+        x_scales = keep.tile([P, PASSES, B], U8, name="x_scales", align_bytes=64)
+
+        def load_x(pair):
+            nc.sync.dma_start(out=x_raw[pair][:], in_=x_v[:, 2 * pair : 2 * pair + 2, :])
+
+        def load_w(nb):
+            for g in range(PASSES):
+                rows = weight[P * PACK * g : P * PACK * g + P * PACK, BLOCK * nb : BLOCK * nb + BLOCK]
+                nc.sync.dma_start(
+                    out=w_raw[nb][:, PACK * g : PACK * g + PACK, :],
+                    in_=rows.rearrange("(q t) n -> q t n", t=PACK),
+                )
+
+        p_rows = const.tile([P, P], BF16, name="p_rows")
+        nc.vector.memset(p_rows[:], 0.0)
+        for v, vec in enumerate((bn_gamma, bn_beta, bn_mean, bn_var)):
+            nc.scalar.dma_start(out=p_rows[16 * v : 16 * v + 16, :], in_=vec.rearrange("(r c) -> r c", c=P))
+        load_x(0)
+        load_x(1)
+        load_w(0)
+        load_x(2)
+        load_x(3)
+        for nb in range(1, N_BLOCKS):
+            load_w(nb)
+
+        ident_f = const.tile([P, P], F32, name="ident_f")
+        make_identity(nc, ident_f[:])
+        ident_b = const.tile([P, P], BF16, name="ident_b")
+        make_identity(nc, ident_b[:])
+        minus_half = const.tile([P, 16], F32, name="minus_half")
+        nc.gpsimd.memset(minus_half[:], -0.5)
+
+        p_cols = const.tile([P, 48], F32, name="p_cols")
+        var_eps = const.tile([P, 16], F32, name="var_eps")
+        rstd = const.tile([P, 16], F32, name="rstd")
+        s_col = const.tile([P, 16], F32, name="s_col")
+        mean_s = const.tile([P, 16], F32, name="mean_s")
+        t_col = const.tile([P, 16], F32, name="t_col")
+        warm_in = const.tile([P, 1], F32, name="warm_in")
+        warm_out = const.tile([P, 1], F32, name="warm_out")
+        nc.vector.memset(warm_in[:], 0.0)
+        tiles = {}
+
+        def load_gelu_table():
+            nc.scalar.activation(out=warm_out[:], in_=warm_in[:], func=ACT.Gelu_apprx_tanh)
+
+        def transpose_params():
+            tiles["params"] = ps_acc.tile([P, P], BF16, name="params", tag="acc")
+            nc.tensor.transpose(tiles["params"][:], p_rows[:], ident_b[:])
+
+        def inverse_std():
+            nc.vector.tensor_copy(out=p_cols[:], in_=tiles["params"][:, 0:48])
+            nc.vector.tensor_scalar_add(var_eps[:], tiles["params"][:, 48:64], EPS)
+            nc.gpsimd.tensor_tensor(out=rstd[:], in0=var_eps[:], in1=minus_half[:], op=ALU.pow)
+
+        def scale_and_shift():
+            nc.vector.tensor_mul(s_col[:], p_cols[:, 0:16], rstd[:])
+            nc.vector.tensor_mul(mean_s[:], p_cols[:, 32:48], s_col[:])
+            nc.vector.tensor_sub(t_col[:], p_cols[:, 16:32], mean_s[:])
+
+        def transpose_x(pair, g):
+            xt = ps_tr.tile([P, 2, 2 * P], F32, name="xt", tag="tr")
+            for u in range(2):
+                for i in range(2):
+                    words = x_raw[pair][:, i, :].bitcast(F32)
+                    every_second = words[:, 2 * P * g + u : 2 * P * g + 2 * P : 2]
+                    nc.tensor.transpose(xt[:, u, P * i : P * i + P], every_second, ident_f[:])
+            tiles["xt", pair, g] = xt
+
+        def copy_x(pair, g, on_scalar):
+            xg = xg_pool.tile([P, PACK * 2 * P], BF16, name="xg", align_bytes=64)
+            dst = xg[:].bitcast(F32).rearrange("p (c u) -> p c u", u=2)
+            src = tiles["xt", pair, g][:].rearrange("p u c -> p c u")
+            if on_scalar:
+                nc.scalar.copy(out=dst, in_=src)
+            else:
+                nc.vector.tensor_copy(out=dst, in_=src)
+            tiles["xg", pair, g] = xg
+
+        def quantise_x(pair, g):
+            cols = slice(2 * P * pair, 2 * P * pair + 2 * P)
+            nc.vector.quantize_mx(
+                out=x_codes[:, g, cols].bitcast(FP8X4), scales=x_scales[:, g, cols], in_=tiles["xg", pair, g][:]
+            )
+
+        def regroup_w(nb, g):
+            wg = wg_pool.tile([P, BLOCK, PACK], BF16, name="wg", align_bytes=64)
+            split = VECTOR_COLS if nb < SHARED_BLOCKS and g > 0 else BLOCK
+            for c0, c1 in ((0, split), (split, BLOCK)):
+                if c0 == c1:
+                    continue
+                dst = wg[:, c0:c1, :].rearrange("p (c i) t -> p c t i", i=4)
+                src = w_raw[nb][:, PACK * g : PACK * g + PACK, c0:c1].rearrange("p t (c i) -> p c t i", i=4)
+                if c0 == 0:
+                    nc.vector.tensor_copy(out=dst, in_=src)
+                else:
+                    nc.scalar.copy(out=dst, in_=src)
+            tiles["wg", nb, g] = wg
+
+        def quantise_w(nb, g):
+            cols = slice(BLOCK * nb, BLOCK * nb + BLOCK)
+            nc.vector.quantize_mx(
+                out=w_codes[:, g, cols].bitcast(FP8X4),
+                scales=w_scales[:, g, cols],
+                in_=tiles["wg", nb, g][:].rearrange("p n t -> p (n t)"),
+            )
+
+        def mx_pass(u, i, g):
+            nb, h = divmod(u, 2)
+            if g == 0:
+                tiles["acc", u, i] = ps_acc.tile([P, HALF], F32, name="acc", tag="acc")
+            n_cols = slice(BLOCK * nb + P * i, BLOCK * nb + P * i + P)
+            b_cols = slice(HALF * h, HALF * h + HALF)
+            nc.tensor.matmul_mx(
+                out=tiles["acc", u, i][:],
+                lhsT=w_codes[:, g, n_cols].bitcast(FP8X4),
+                lhsT_scale=w_scales[:, g, n_cols],
+                rhs=x_codes[:, g, b_cols].bitcast(FP8X4),
+                rhs_scale=x_scales[:, g, b_cols],
+                start=(g == 0),
+                stop=(g == PASSES - 1),
+            )
+
+        def multiply(u, i):
+            for g in range(PASSES):
+                mx_pass(u, i, g)
+
+        def first_exit(u, i):
+            col = COL_TILES * (u // 2) + i
+            g_t = g_pool.tile([P, HALF], F32, name="g_t")
+            nc.scalar.activation(
+                out=g_t[:],
+                in_=tiles["acc", u, i][:],
+                func=(ACT.Gelu_apprx_tanh if i % 2 == 0 else ACT.Relu),
+                bias=t_col[:, col : col + 1],
+                scale=s_col[:, col : col + 1],
+            )
+            tiles["g", u, i] = g_t
+
+        def turn_back(u, i):
+            tb = ps_tr.tile([P, HALF_TILES, P], F32, name="tb", tag="tr")
+            for tt in range(HALF_TILES):
+                nc.tensor.transpose(tb[:, tt, :], tiles["g", u, i][:, P * tt : P * tt + P], ident_f[:])
+            tiles["tb", u, i] = tb
+
+        def second_exit(u, i):
+            if i == 0:
+                tiles["o", u] = o_pool.tile([P, HALF_TILES, BLOCK], F32, name="o_sb")
+            dst = tiles["o", u][:, :, P * i : P * i + P]
+            if i % 2 == 0:
+                nc.vector.tensor_scalar(dst, tiles["tb", u, i][:], 0.0, 0.0, op0=ALU.max, op1=ALU.add)
+            else:
+                nc.scalar.activation(out=dst, in_=tiles["tb", u, i][:], func=ACT.Gelu_apprx_tanh)
+
+        def finish(u, i):
+            turn_back(u, i)
+            second_exit(u, i)
+
+        def store(u, i0, i1):
+            nb, h = divmod(u, 2)
+            nc.sync.dma_start(
+                out=out_v[:, HALF_TILES * h : HALF_TILES * h + HALF_TILES, BLOCK * nb + P * i0 : BLOCK * nb + P * i1],
+                in_=tiles["o", u][:, :, P * i0 : P * i1],
+            )
+
+        load_gelu_table()
+        for g in range(PASSES):
+            transpose_x(0, g)
+        transpose_params()
+        for g in range(PASSES):
+            copy_x(0, g, True)
+            quantise_x(0, g)
+        inverse_std()
+        for g in range(PASSES):
+            transpose_x(1, g)
+        for g in range(PASSES):
+            copy_x(1, g, True)
+
+        for g in range(PASSES):
+            regroup_w(0, g)
+            quantise_x(1, g)
+            quantise_w(0, g)
+            if g == PASSES - 1:
+                scale_and_shift()
+                for gg in range(PASSES):
+                    transpose_x(2, gg)
+            for i in range(COL_TILES):
+                mx_pass(0, i, g)
+
+        for pair in (2, 3):
+            if pair == 3:
+                for g in range(PASSES):
+                    transpose_x(3, g)
+                turn_back(0, 0)
+                turn_back(0, 1)
+            for g in range(PASSES):
+                copy_x(pair, g, g % 2 == 1)
+            for g in range(PASSES):
+                quantise_x(pair, g)
+            first_exit(0, 2 * pair - 4)
+            first_exit(0, 2 * pair - 3)
+
+        for i in range(COL_TILES):
+            multiply(1, i)
+        turn_back(0, 2)
+        turn_back(0, 3)
+        regroup_w(1, 0)
+        for g in range(1, PASSES):
+            regroup_w(1, g)
+            quantise_w(1, g - 1)
+        quantise_w(1, PASSES - 1)
+        for i in range(COL_TILES):
+            first_exit(1, i)
+        for i in range(COL_TILES):
+            second_exit(0, i)
+        store(0, 0, COL_TILES)
+
+        for u in range(2, LAST):
+            nb, h = divmod(u, 2)
+            for i in range(COL_TILES):
+                multiply(u, i)
+                first_exit(u, i)
+            if nb + 1 < N_BLOCKS:
+                regroup_w(nb + 1, 2 * h)
+                regroup_w(nb + 1, 2 * h + 1)
+                quantise_w(nb + 1, 2 * h)
+                quantise_w(nb + 1, 2 * h + 1)
+            for i in range(COL_TILES):
+                finish(u - 1, i)
+            store(u - 1, 0, COL_TILES)
+
+        multiply(LAST, 0)
+        first_exit(LAST, 0)
+        for i in range(COL_TILES):
+            finish(LAST - 1, i)
+        store(LAST - 1, 0, COL_TILES)
+        multiply(LAST, 1)
+        first_exit(LAST, 1)
+        multiply(LAST, 2)
+        first_exit(LAST, 2)
+        finish(LAST, 0)
+        finish(LAST, 1)
+        store(LAST, 0, 2)
+        multiply(LAST, 3)
+        first_exit(LAST, 3)
+        finish(LAST, 2)
+        store(LAST, 2, 3)
+        finish(LAST, 3)
+        store(LAST, 3, 4)

@@ -27,35 +27,28 @@ BLOCK = COL_TILES * P
 N_BLOCKS = N // BLOCK
 UNITS = 2 * N_BLOCKS
 LAST = UNITS - 1
-SHARED_BLOCKS = 2
-VECTOR_COLS = BLOCK // 2
 
 
 def tile_modelnew_kernel(tc, x, weight, bn_gamma, bn_beta, bn_mean, bn_var, out):
     nc = tc.nc
-    x_v = x.rearrange("(p t) k -> p t k", t=ROW_TILES)
-    out_v = out.rearrange("(p t) n -> p t n", t=ROW_TILES)
+    out_v = out.rearrange("(t p) n -> p t n", p=P)
 
     with ExitStack() as ctx:
         const = ctx.enter_context(tc.tile_pool(name="const", bufs=1))
         keep = ctx.enter_context(tc.tile_pool(name="keep", bufs=1))
-        wg_pool = ctx.enter_context(tc.tile_pool(name="wg_pool", bufs=3))
-        xg_pool = ctx.enter_context(tc.tile_pool(name="xg_pool", bufs=2 * PASSES))
-        g_pool = ctx.enter_context(tc.tile_pool(name="g_pool", bufs=2 * COL_TILES))
+        wg_pool = ctx.enter_context(tc.tile_pool(name="wg_pool", bufs=4))
+        xg_pool = ctx.enter_context(tc.tile_pool(name="xg_pool", bufs=2))
+        g_pool = ctx.enter_context(tc.tile_pool(name="g_pool", bufs=3 * COL_TILES))
         o_pool = ctx.enter_context(tc.tile_pool(name="o_pool", bufs=3))
-        ps_acc = ctx.enter_context(tc.psum_pool(name="ps_acc", bufs=4))
-        ps_tr = ctx.enter_context(tc.psum_pool(name="ps_tr", bufs=4))
+        banks = ctx.enter_context(tc.psum_pool(name="banks", bufs=8))
         ctx.enter_context(tc.manual_schedule())
 
-        x_raw = [keep.tile([P, 2, K], BF16, name="x_raw%d" % pair) for pair in range(PAIRS)]
+        x_raw = [keep.tile([P, K], BF16, name="x_raw%d" % t) for t in range(ROW_TILES)]
         w_raw = [keep.tile([P, PACK * PASSES, BLOCK], BF16, name="w_raw%d" % nb) for nb in range(N_BLOCKS)]
         w_codes = keep.tile([P, PASSES, N], U32, name="w_codes", align_bytes=64)
         w_scales = keep.tile([P, PASSES, N], U8, name="w_scales", align_bytes=64)
         x_codes = keep.tile([P, PASSES, B], U32, name="x_codes", align_bytes=64)
         x_scales = keep.tile([P, PASSES, B], U8, name="x_scales", align_bytes=64)
-
-        def load_x(pair):
-            nc.sync.dma_start(out=x_raw[pair][:], in_=x_v[:, 2 * pair : 2 * pair + 2, :])
 
         def load_w(nb):
             for g in range(PASSES):
@@ -69,12 +62,9 @@ def tile_modelnew_kernel(tc, x, weight, bn_gamma, bn_beta, bn_mean, bn_var, out)
         nc.vector.memset(p_rows[:], 0.0)
         for v, vec in enumerate((bn_gamma, bn_beta, bn_mean, bn_var)):
             nc.scalar.dma_start(out=p_rows[16 * v : 16 * v + 16, :], in_=vec.rearrange("(r c) -> r c", c=P))
-        load_x(0)
-        load_x(1)
-        load_w(0)
-        load_x(2)
-        load_x(3)
-        for nb in range(1, N_BLOCKS):
+        for t in range(ROW_TILES):
+            nc.sync.dma_start(out=x_raw[t][:], in_=x[P * t : P * t + P, :])
+        for nb in range(N_BLOCKS):
             load_w(nb)
 
         ident_f = const.tile([P, P], F32, name="ident_f")
@@ -99,7 +89,7 @@ def tile_modelnew_kernel(tc, x, weight, bn_gamma, bn_beta, bn_mean, bn_var, out)
             nc.scalar.activation(out=warm_out[:], in_=warm_in[:], func=ACT.Gelu_apprx_tanh)
 
         def transpose_params():
-            tiles["params"] = ps_acc.tile([P, P], BF16, name="params", tag="acc")
+            tiles["params"] = banks.tile([P, P], BF16, name="params", tag="bank")
             nc.tensor.transpose(tiles["params"][:], p_rows[:], ident_b[:])
 
         def inverse_std():
@@ -112,43 +102,41 @@ def tile_modelnew_kernel(tc, x, weight, bn_gamma, bn_beta, bn_mean, bn_var, out)
             nc.vector.tensor_mul(mean_s[:], p_cols[:, 32:48], s_col[:])
             nc.vector.tensor_sub(t_col[:], p_cols[:, 16:32], mean_s[:])
 
-        def transpose_x(pair, g):
-            xt = ps_tr.tile([P, 2, 2 * P], F32, name="xt", tag="tr")
-            for u in range(2):
-                for i in range(2):
-                    words = x_raw[pair][:, i, :].bitcast(F32)
-                    every_second = words[:, 2 * P * g + u : 2 * P * g + 2 * P : 2]
-                    nc.tensor.transpose(xt[:, u, P * i : P * i + P], every_second, ident_f[:])
-            tiles["xt", pair, g] = xt
+        def transpose_x(t, gg):
+            xt = banks.tile([P, 2, 2, P], F32, name="xt", tag="bank")
+            words = x_raw[t][:].bitcast(F32)
+            for e in range(2):
+                for u in range(2):
+                    g = 2 * gg + e
+                    nc.tensor.transpose(xt[:, e, u, :], words[:, 2 * P * g + u : 2 * P * g + 2 * P : 2], ident_f[:])
+            tiles["xt", t, gg] = xt
 
-        def copy_x(pair, g, on_scalar):
-            xg = xg_pool.tile([P, PACK * 2 * P], BF16, name="xg", align_bytes=64)
-            dst = xg[:].bitcast(F32).rearrange("p (c u) -> p c u", u=2)
-            src = tiles["xt", pair, g][:].rearrange("p u c -> p c u")
-            if on_scalar:
-                nc.scalar.copy(out=dst, in_=src)
-            else:
-                nc.vector.tensor_copy(out=dst, in_=src)
-            tiles["xg", pair, g] = xg
+        def copy_x(t, gg, on_scalar):
+            pair, odd = divmod(t, 2)
+            if odd == 0 and gg == 0:
+                tiles["xg", pair] = xg_pool.tile([P, PASSES, 2 * P * PACK], BF16, name="xg", align_bytes=64)
+            cols = tiles["xg", pair][:, 2 * gg : 2 * gg + 2, P * PACK * odd : P * PACK * odd + P * PACK]
+            dst = cols.bitcast(F32).rearrange("p g (c u) -> p g c u", u=2)
+            src = tiles["xt", t, gg][:].rearrange("p g u c -> p g c u")
+            (nc.scalar.copy if on_scalar else nc.vector.tensor_copy)(out=dst, in_=src)
 
-        def quantise_x(pair, g):
-            cols = slice(2 * P * pair, 2 * P * pair + 2 * P)
+        def quantise_x(pair, g, c0=0, c1=2):
+            cols = slice(2 * P * pair + P * c0, 2 * P * pair + P * c1)
             nc.vector.quantize_mx(
-                out=x_codes[:, g, cols].bitcast(FP8X4), scales=x_scales[:, g, cols], in_=tiles["xg", pair, g][:]
+                out=x_codes[:, g, cols].bitcast(FP8X4),
+                scales=x_scales[:, g, cols],
+                in_=tiles["xg", pair][:, g, P * PACK * c0 : P * PACK * c1],
             )
 
-        def regroup_w(nb, g):
+        def regroup_w(nb, g, by_scalar):
             wg = wg_pool.tile([P, BLOCK, PACK], BF16, name="wg", align_bytes=64)
-            split = VECTOR_COLS if nb < SHARED_BLOCKS and g > 0 else BLOCK
-            for c0, c1 in ((0, split), (split, BLOCK)):
+            split = BLOCK - P * by_scalar
+            for c0, c1, engine_copy in ((0, split, nc.vector.tensor_copy), (split, BLOCK, nc.scalar.copy)):
                 if c0 == c1:
                     continue
                 dst = wg[:, c0:c1, :].rearrange("p (c i) t -> p c t i", i=4)
                 src = w_raw[nb][:, PACK * g : PACK * g + PACK, c0:c1].rearrange("p t (c i) -> p c t i", i=4)
-                if c0 == 0:
-                    nc.vector.tensor_copy(out=dst, in_=src)
-                else:
-                    nc.scalar.copy(out=dst, in_=src)
+                engine_copy(out=dst, in_=src)
             tiles["wg", nb, g] = wg
 
         def quantise_w(nb, g):
@@ -162,7 +150,7 @@ def tile_modelnew_kernel(tc, x, weight, bn_gamma, bn_beta, bn_mean, bn_var, out)
         def mx_pass(u, i, g):
             nb, h = divmod(u, 2)
             if g == 0:
-                tiles["acc", u, i] = ps_acc.tile([P, HALF], F32, name="acc", tag="acc")
+                tiles["acc", u, i] = banks.tile([P, HALF], F32, name="acc", tag="bank")
             n_cols = slice(BLOCK * nb + P * i, BLOCK * nb + P * i + P)
             b_cols = slice(HALF * h, HALF * h + HALF)
             nc.tensor.matmul_mx(
@@ -185,30 +173,26 @@ def tile_modelnew_kernel(tc, x, weight, bn_gamma, bn_beta, bn_mean, bn_var, out)
             nc.scalar.activation(
                 out=g_t[:],
                 in_=tiles["acc", u, i][:],
-                func=(ACT.Gelu_apprx_tanh if i % 2 == 0 else ACT.Relu),
+                func=ACT.Gelu_apprx_tanh,
                 bias=t_col[:, col : col + 1],
                 scale=s_col[:, col : col + 1],
             )
             tiles["g", u, i] = g_t
 
         def turn_back(u, i):
-            tb = ps_tr.tile([P, HALF_TILES, P], F32, name="tb", tag="tr")
+            tb = banks.tile([P, HALF_TILES, P], F32, name="tb", tag="bank")
             for tt in range(HALF_TILES):
                 nc.tensor.transpose(tb[:, tt, :], tiles["g", u, i][:, P * tt : P * tt + P], ident_f[:])
             tiles["tb", u, i] = tb
 
-        def second_exit(u, i):
+        def second_exit(u, i, on_scalar):
             if i == 0:
                 tiles["o", u] = o_pool.tile([P, HALF_TILES, BLOCK], F32, name="o_sb")
             dst = tiles["o", u][:, :, P * i : P * i + P]
-            if i % 2 == 0:
+            if not on_scalar:
                 nc.vector.tensor_scalar(dst, tiles["tb", u, i][:], 0.0, 0.0, op0=ALU.max, op1=ALU.add)
             else:
-                nc.scalar.activation(out=dst, in_=tiles["tb", u, i][:], func=ACT.Gelu_apprx_tanh)
-
-        def finish(u, i):
-            turn_back(u, i)
-            second_exit(u, i)
+                nc.scalar.activation(out=dst, in_=tiles["tb", u, i][:], func=ACT.Relu)
 
         def store(u, i0, i1):
             nb, h = divmod(u, 2)
@@ -218,86 +202,75 @@ def tile_modelnew_kernel(tc, x, weight, bn_gamma, bn_beta, bn_mean, bn_var, out)
             )
 
         load_gelu_table()
-        for g in range(PASSES):
-            transpose_x(0, g)
-        transpose_params()
-        for g in range(PASSES):
-            copy_x(0, g, True)
-            quantise_x(0, g)
-        inverse_std()
-        for g in range(PASSES):
-            transpose_x(1, g)
-        for g in range(PASSES):
-            copy_x(1, g, True)
-
-        for g in range(PASSES):
-            regroup_w(0, g)
-            quantise_x(1, g)
-            quantise_w(0, g)
-            if g == PASSES - 1:
-                scale_and_shift()
-                for gg in range(PASSES):
-                    transpose_x(2, gg)
-            for i in range(COL_TILES):
-                mx_pass(0, i, g)
-
-        for pair in (2, 3):
-            if pair == 3:
+        for t in range(ROW_TILES):
+            for gg in range(2):
+                transpose_x(t, gg)
+            for gg in range(2):
+                copy_x(t, gg, gg == 1 or t in (2, 4, 6))
+            if t == 1:
+                transpose_params()
+            if t % 2 and t < 7:
                 for g in range(PASSES):
-                    transpose_x(3, g)
-                turn_back(0, 0)
-                turn_back(0, 1)
-            for g in range(PASSES):
-                copy_x(pair, g, g % 2 == 1)
-            for g in range(PASSES):
-                quantise_x(pair, g)
-            first_exit(0, 2 * pair - 4)
-            first_exit(0, 2 * pair - 3)
-
-        for i in range(COL_TILES):
-            multiply(1, i)
-        turn_back(0, 2)
-        turn_back(0, 3)
-        regroup_w(1, 0)
+                    quantise_x(t // 2, g)
+            if t == 3:
+                inverse_std()
+        regroup_w(0, 0, 2)
+        for g in range(PASSES):
+            quantise_x(3, g)
+            if g + 1 < PASSES:
+                regroup_w(0, g + 1, 2)
+            else:
+                scale_and_shift()
+                regroup_w(1, 0, 2)
+            quantise_w(0, g)
+            for u in range(2):
+                for i in range(COL_TILES):
+                    mx_pass(u, i, g)
         for g in range(1, PASSES):
-            regroup_w(1, g)
+            regroup_w(1, g, 2)
             quantise_w(1, g - 1)
-        quantise_w(1, PASSES - 1)
-        for i in range(COL_TILES):
-            first_exit(1, i)
-        for i in range(COL_TILES):
-            second_exit(0, i)
-        store(0, 0, COL_TILES)
+        quantise_w(1, 3)
+        for u in range(2):
+            for i in range(COL_TILES):
+                first_exit(u, i)
 
+        def finish(f):
+            for i in range(COL_TILES):
+                turn_back(f, i)
+            for i in range(COL_TILES):
+                second_exit(f, i, i % 2 == 1)
+            store(f, 0, COL_TILES)
+
+        behind = {2: (0,), 3: (1,), 4: (2,), 5: (3,4), 6: (5,)}
         for u in range(2, LAST):
             nb, h = divmod(u, 2)
+            if nb + 1 < N_BLOCKS:
+                regroup_w(nb + 1, 2 * h, 1)
+                regroup_w(nb + 1, 2 * h + 1, 1)
             for i in range(COL_TILES):
                 multiply(u, i)
                 first_exit(u, i)
             if nb + 1 < N_BLOCKS:
-                regroup_w(nb + 1, 2 * h)
-                regroup_w(nb + 1, 2 * h + 1)
                 quantise_w(nb + 1, 2 * h)
                 quantise_w(nb + 1, 2 * h + 1)
-            for i in range(COL_TILES):
-                finish(u - 1, i)
-            store(u - 1, 0, COL_TILES)
-
+            for f in behind[u]:
+                finish(f)
         multiply(LAST, 0)
         first_exit(LAST, 0)
-        for i in range(COL_TILES):
-            finish(LAST - 1, i)
-        store(LAST - 1, 0, COL_TILES)
+        finish(6)
         multiply(LAST, 1)
         first_exit(LAST, 1)
         multiply(LAST, 2)
         first_exit(LAST, 2)
-        finish(LAST, 0)
-        finish(LAST, 1)
+        for i in range(2):
+            turn_back(LAST, i)
+            second_exit(LAST, i, i % 2 == 1)
         store(LAST, 0, 2)
         multiply(LAST, 3)
         first_exit(LAST, 3)
-        finish(LAST, 2)
+        turn_back(LAST, 2)
+        second_exit(LAST, 2, False)
         store(LAST, 2, 3)
-        finish(LAST, 3)
+        turn_back(LAST, 3)
+        second_exit(LAST, 3, True)
         store(LAST, 3, 4)

@@ -25,6 +25,7 @@ HALF = HALF_TILES * P
 COL_TILES = 4
 BLOCK = COL_TILES * P
 N_BLOCKS = N // BLOCK
+ROW_N0 = 2 * BLOCK
 UNITS = 2 * N_BLOCKS
 LAST = UNITS - 1
 
@@ -37,21 +38,26 @@ def tile_modelnew_kernel(tc, x, weight, bn_gamma, bn_beta, bn_mean, bn_var, out)
         const = ctx.enter_context(tc.tile_pool(name="const", bufs=1))
         keep = ctx.enter_context(tc.tile_pool(name="keep", bufs=1))
         wg_pool = ctx.enter_context(tc.tile_pool(name="wg_pool", bufs=4))
+        wr_pool = ctx.enter_context(tc.tile_pool(name="wr_pool", bufs=3))
         xg_pool = ctx.enter_context(tc.tile_pool(name="xg_pool", bufs=2))
         g_pool = ctx.enter_context(tc.tile_pool(name="g_pool", bufs=3 * COL_TILES))
         o_pool = ctx.enter_context(tc.tile_pool(name="o_pool", bufs=3))
-        banks = ctx.enter_context(tc.psum_pool(name="banks", bufs=8))
+        row_pool = ctx.enter_context(tc.tile_pool(name="row_pool", bufs=1))
+        ps_acc = ctx.enter_context(tc.psum_pool(name="ps_acc", bufs=4))
+        ps_tr = ctx.enter_context(tc.psum_pool(name="ps_tr", bufs=4))
         ctx.enter_context(tc.manual_schedule())
 
         x_raw = [keep.tile([P, K], BF16, name="x_raw%d" % t) for t in range(ROW_TILES)]
-        w_raw = [keep.tile([P, PACK * PASSES, BLOCK], BF16, name="w_raw%d" % nb) for nb in range(N_BLOCKS)]
+        w_raw = {}
         w_codes = keep.tile([P, PASSES, N], U32, name="w_codes", align_bytes=64)
         w_scales = keep.tile([P, PASSES, N], U8, name="w_scales", align_bytes=64)
         x_codes = keep.tile([P, PASSES, B], U32, name="x_codes", align_bytes=64)
         x_scales = keep.tile([P, PASSES, B], U8, name="x_scales", align_bytes=64)
 
-        def load_w(nb):
-            for g in range(PASSES):
+        def load_w(nb, g0=0, g1=PASSES):
+            if g0 == 0:
+                w_raw[nb] = wr_pool.tile([P, PACK * PASSES, BLOCK], BF16, name="w_raw")
+            for g in range(g0, g1):
                 rows = weight[P * PACK * g : P * PACK * g + P * PACK, BLOCK * nb : BLOCK * nb + BLOCK]
                 nc.sync.dma_start(
                     out=w_raw[nb][:, PACK * g : PACK * g + PACK, :],
@@ -59,13 +65,16 @@ def tile_modelnew_kernel(tc, x, weight, bn_gamma, bn_beta, bn_mean, bn_var, out)
                 )
 
         p_rows = const.tile([P, P], BF16, name="p_rows")
-        nc.vector.memset(p_rows[:], 0.0)
-        for v, vec in enumerate((bn_gamma, bn_beta, bn_mean, bn_var)):
-            nc.scalar.dma_start(out=p_rows[16 * v : 16 * v + 16, :], in_=vec.rearrange("(r c) -> r c", c=P))
+        nc.vector.memset(p_rows[64:P, :], 0.0)
         for t in range(ROW_TILES):
             nc.sync.dma_start(out=x_raw[t][:], in_=x[P * t : P * t + P, :])
-        for nb in range(N_BLOCKS):
-            load_w(nb)
+            if t == 0:
+                for v, vec in enumerate((bn_gamma, bn_beta, bn_mean, bn_var)):
+                    nc.sync.dma_start(out=p_rows[16 * v : 16 * v + 16, :], in_=vec.rearrange("(r c) -> r c", c=P))
+            for g in {7: (0, 1, 2, 3)}.get(t, ()):
+                load_w(0, g, g + 1)
+        load_w(1)
+        load_w(2)
 
         ident_f = const.tile([P, P], F32, name="ident_f")
         make_identity(nc, ident_f[:])
@@ -77,9 +86,11 @@ def tile_modelnew_kernel(tc, x, weight, bn_gamma, bn_beta, bn_mean, bn_var, out)
         p_cols = const.tile([P, 48], F32, name="p_cols")
         var_eps = const.tile([P, 16], F32, name="var_eps")
         rstd = const.tile([P, 16], F32, name="rstd")
-        s_col = const.tile([P, 16], F32, name="s_col")
+        st_cols = const.tile([P, P], F32, name="st_cols")
+        s_col = st_cols[:, 0:16]
+        t_col = st_cols[:, 16:32]
         mean_s = const.tile([P, 16], F32, name="mean_s")
-        t_col = const.tile([P, 16], F32, name="t_col")
+        nc.gpsimd.memset(st_cols[:, 32:P], 0.0)
         warm_in = const.tile([P, 1], F32, name="warm_in")
         warm_out = const.tile([P, 1], F32, name="warm_out")
         nc.vector.memset(warm_in[:], 0.0)
@@ -89,7 +100,7 @@ def tile_modelnew_kernel(tc, x, weight, bn_gamma, bn_beta, bn_mean, bn_var, out)
             nc.scalar.activation(out=warm_out[:], in_=warm_in[:], func=ACT.Gelu_apprx_tanh)
 
         def transpose_params():
-            tiles["params"] = banks.tile([P, P], BF16, name="params", tag="bank")
+            tiles["params"] = ps_tr.tile([P, P], BF16, name="params", tag="bank")
             nc.tensor.transpose(tiles["params"][:], p_rows[:], ident_b[:])
 
         def inverse_std():
@@ -98,12 +109,12 @@ def tile_modelnew_kernel(tc, x, weight, bn_gamma, bn_beta, bn_mean, bn_var, out)
             nc.gpsimd.tensor_tensor(out=rstd[:], in0=var_eps[:], in1=minus_half[:], op=ALU.pow)
 
         def scale_and_shift():
-            nc.vector.tensor_mul(s_col[:], p_cols[:, 0:16], rstd[:])
-            nc.vector.tensor_mul(mean_s[:], p_cols[:, 32:48], s_col[:])
-            nc.vector.tensor_sub(t_col[:], p_cols[:, 16:32], mean_s[:])
+            nc.vector.tensor_mul(s_col, p_cols[:, 0:16], rstd[:])
+            nc.vector.tensor_mul(mean_s[:], p_cols[:, 32:48], s_col)
+            nc.vector.tensor_sub(t_col, p_cols[:, 16:32], mean_s[:])
 
         def transpose_x(t, gg):
-            xt = banks.tile([P, 2, 2, P], F32, name="xt", tag="bank")
+            xt = ps_tr.tile([P, 2, 2, P], F32, name="xt", tag="bank")
             words = x_raw[t][:].bitcast(F32)
             for e in range(2):
                 for u in range(2):
@@ -150,7 +161,7 @@ def tile_modelnew_kernel(tc, x, weight, bn_gamma, bn_beta, bn_mean, bn_var, out)
         def mx_pass(u, i, g):
             nb, h = divmod(u, 2)
             if g == 0:
-                tiles["acc", u, i] = banks.tile([P, HALF], F32, name="acc", tag="bank")
+                tiles["acc", u, i] = (ps_tr if u == 1 else ps_acc).tile([P, HALF], F32, name="acc", tag="bank")
             n_cols = slice(BLOCK * nb + P * i, BLOCK * nb + P * i + P)
             b_cols = slice(HALF * h, HALF * h + HALF)
             nc.tensor.matmul_mx(
@@ -179,8 +190,67 @@ def tile_modelnew_kernel(tc, x, weight, bn_gamma, bn_beta, bn_mean, bn_var, out)
             )
             tiles["g", u, i] = g_t
 
+        def park():
+            bank = ps_tr.tile([P, P], F32, name="st_bank", tag="bank")
+            nc.tensor.transpose(bank[:], st_cols[:], ident_f[:])
+            st_rows = const.tile([32, P], F32, name="st_rows")
+            nc.scalar.copy(out=st_rows[:], in_=bank[0:32, :])
+            nc.sync.dma_start(out=out[B - 2 : B, :].rearrange("v (r c) -> (v r) c", c=P), in_=st_rows[:])
+            for name, row in (("s", B - 2), ("t", B - 1)):
+                wide = row_pool.tile([P, N - ROW_N0], F32, name="row_" + name)
+                nc.sync.dma_start(out=wide[:], in_=out[row, ROW_N0:N].partition_broadcast(P))
+                tiles[name] = wide
+
+        def row_of(name, nb):
+            return tiles[name][:, BLOCK * nb - ROW_N0 : BLOCK * nb - ROW_N0 + BLOCK]
+
+        def multiply_rows(u, r):
+            nb, h = divmod(u, 2)
+            acc = ps_acc.tile([P, BLOCK], F32, name="acc_r", tag="bank")
+            rows = slice(HALF * h + P * r, HALF * h + P * r + P)
+            n_cols = slice(BLOCK * nb, BLOCK * nb + BLOCK)
+            for g in range(PASSES):
+                nc.tensor.matmul_mx(
+                    out=acc[:],
+                    lhsT=x_codes[:, g, rows].bitcast(FP8X4),
+                    lhsT_scale=x_scales[:, g, rows],
+                    rhs=w_codes[:, g, n_cols].bitcast(FP8X4),
+                    rhs_scale=w_scales[:, g, n_cols],
+                    start=(g == 0),
+                    stop=(g == PASSES - 1),
+                )
+            tiles["acc", u, r] = acc
+
+        def scale_rows(u, r):
+            y = g_pool.tile([P, BLOCK], F32, name="g_t")
+            nc.vector.tensor_tensor(out=y[:], in0=tiles["acc", u, r][:], in1=row_of("s", u // 2), op=ALU.mult)
+            tiles["y", u, r] = y
+
+        def shift_rows(u, r):
+            y = tiles["y", u, r]
+            nc.vector.tensor_tensor(out=y[:], in0=y[:], in1=row_of("t", u // 2), op=ALU.add)
+
+        def gelu_rows(u, r):
+            if r == 0:
+                tiles["o", u] = o_pool.tile([P, HALF_TILES, BLOCK], F32, name="o_sb")
+            nc.scalar.activation(out=tiles["o", u][:, r, :], in_=tiles["y", u, r][:], func=ACT.Gelu_apprx_tanh)
+
+        def relu_rows(u, r0, r1, on_scalar=False):
+            part = tiles["o", u][:, r0:r1, :]
+            if on_scalar:
+                nc.scalar.activation(out=part, in_=part, func=ACT.Relu)
+            else:
+                nc.vector.tensor_scalar(part, part, 0.0, 0.0, op0=ALU.max, op1=ALU.add)
+
+        def store_rows(u, r0, r1):
+            nb, h = divmod(u, 2)
+            nc.sync.dma_start(
+                out=out_v[:, HALF_TILES * h + r0 : HALF_TILES * h + r1, BLOCK * nb : BLOCK * nb + BLOCK],
+                in_=tiles["o", u][:, r0:r1, :],
+            )
+
         def turn_back(u, i):
-            tb = banks.tile([P, HALF_TILES, P], F32, name="tb", tag="bank")
+            tb = ps_tr.tile([P, HALF_TILES, P], F32, name="tb", tag="bank")
             for tt in range(HALF_TILES):
                 nc.tensor.transpose(tb[:, tt, :], tiles["g", u, i][:, P * tt : P * tt + P], ident_f[:])
             tiles["tb", u, i] = tb
@@ -202,62 +272,137 @@ def tile_modelnew_kernel(tc, x, weight, bn_gamma, bn_beta, bn_mean, bn_var, out)
             )
 
         load_gelu_table()
+
+        def tx(t):
+            transpose_x(t, 0)
+            transpose_x(t, 1)
+
+        def cx(t, both_scalar):
+            copy_x(t, 0, both_scalar)
+            copy_x(t, 1, True)
+
+        def qx(pair):
+            for g in range(PASSES):
+                quantise_x(pair, g)
+
+        def mx4(u, g):
+            for i in range(COL_TILES):
+                mx_pass(u, i, g)
+
         for t in range(ROW_TILES):
-            for gg in range(2):
-                transpose_x(t, gg)
-            for gg in range(2):
-                copy_x(t, gg, gg == 1 or t in (2, 4, 6))
+            tx(t)
+            cx(t, t in (2, 4, 6))
             if t == 1:
                 transpose_params()
             if t % 2 and t < 7:
-                for g in range(PASSES):
-                    quantise_x(t // 2, g)
-            if t == 3:
+                qx(t // 2)
+            if t == 2:
                 inverse_std()
+            if t == 5:
+                scale_and_shift()
+        park()
         regroup_w(0, 0, 2)
         for g in range(PASSES):
             quantise_x(3, g)
             if g + 1 < PASSES:
                 regroup_w(0, g + 1, 2)
             else:
-                scale_and_shift()
                 regroup_w(1, 0, 2)
             quantise_w(0, g)
-            for u in range(2):
-                for i in range(COL_TILES):
-                    mx_pass(u, i, g)
+            mx4(0, g)
+            mx4(1, g)
+        load_w(3)
         for g in range(1, PASSES):
-            regroup_w(1, g, 2)
+            regroup_w(1, g, (2,2,2,2)[g])
             quantise_w(1, g - 1)
+        regroup_w(2, 0, (0,0,1,2)[0])
         quantise_w(1, 3)
+        regroup_w(2, 1, (0,0,1,2)[1])
+        quantise_w(2, 0)
         for u in range(2):
             for i in range(COL_TILES):
                 first_exit(u, i)
 
-        def finish(f):
+        def part(u, k0, k1):
+            for k in range(k0, k1):
+                multiply(u, k)
+                first_exit(u, k)
+
+        def back(f):
             for i in range(COL_TILES):
                 turn_back(f, i)
+
+        def second(f, by_scalar):
             for i in range(COL_TILES):
-                second_exit(f, i, i % 2 == 1)
+                second_exit(f, i, i in by_scalar)
             store(f, 0, COL_TILES)
 
-        behind = {2: (0,), 3: (1,), 4: (2,), 5: (3,4), 6: (5,)}
-        for u in range(2, LAST):
-            nb, h = divmod(u, 2)
-            if nb + 1 < N_BLOCKS:
-                regroup_w(nb + 1, 2 * h, 1)
-                regroup_w(nb + 1, 2 * h + 1, 1)
-            for i in range(COL_TILES):
-                multiply(u, i)
-                first_exit(u, i)
-            if nb + 1 < N_BLOCKS:
-                quantise_w(nb + 1, 2 * h)
-                quantise_w(nb + 1, 2 * h + 1)
-            for f in behind[u]:
-                finish(f)
+        part(2, 0, 2)
+        regroup_w(2, 2, (0,0,1,2)[2])
+        quantise_w(2, 1)
+        part(2, 2, 4)
+        regroup_w(2, 3, (0,0,1,2)[3])
+        quantise_w(2, 2)
+        back(0)
+        second(0, (3,))
+        quantise_w(2, 3)
+        regroup_w(3, 0, (2,1,1,1)[0])
+        part(3, 0, 2)
+        regroup_w(3, 1, (2,1,1,1)[1])
+        quantise_w(3, 0)
+        part(3, 2, 4)
+        regroup_w(3, 2, (2,1,1,1)[2])
+        quantise_w(3, 1)
+        back(1)
+        second(1, (1, 3))
+        regroup_w(3, 3, (2,1,1,1)[3])
+        quantise_w(3, 2)
+        for r in range(HALF_TILES):
+            multiply_rows(4, r)
+        scale_rows(4, 0)
+        scale_rows(4, 1)
+        quantise_w(3, 3)
+        shift_rows(4, 0)
+        gelu_rows(4, 0)
+        shift_rows(4, 1)
+        gelu_rows(4, 1)
+        scale_rows(4, 2)
+        scale_rows(4, 3)
+        relu_rows(4, 0, 2)
+        store_rows(4, 0, 2)
+        shift_rows(4, 2)
+        gelu_rows(4, 2)
+        shift_rows(4, 3)
+        gelu_rows(4, 3)
+        back(2)
+        second(2, (1, 3))
+        relu_rows(4, 2, 4)
+        store_rows(4, 2, 4)
+        part(5, 0, 4)
+        back(3)
+        second(3, (1, 3))
+        for r in range(HALF_TILES):
+            multiply_rows(6, r)
+        scale_rows(6, 0)
+        scale_rows(6, 1)
+        shift_rows(6, 0)
+        gelu_rows(6, 0)
+        shift_rows(6, 1)
+        gelu_rows(6, 1)
+        scale_rows(6, 2)
+        scale_rows(6, 3)
+        back(5)
+        second(5, (1, 3))
+        relu_rows(6, 0, 2)
+        store_rows(6, 0, 2)
+        shift_rows(6, 2)
+        gelu_rows(6, 2)
+        shift_rows(6, 3)
+        gelu_rows(6, 3)
         multiply(LAST, 0)
         first_exit(LAST, 0)
-        finish(6)
+        relu_rows(6, 2, 4)
+        store_rows(6, 2, 4)
         multiply(LAST, 1)
         first_exit(LAST, 1)
         multiply(LAST, 2)

@@ -25,7 +25,6 @@ HALF = HALF_TILES * P
 COL_TILES = 4
 BLOCK = COL_TILES * P
 N_BLOCKS = N // BLOCK
-ROW_N0 = 2 * BLOCK
 UNITS = 2 * N_BLOCKS
 LAST = UNITS - 1
 
@@ -86,11 +85,9 @@ def tile_modelnew_kernel(tc, x, weight, bn_gamma, bn_beta, bn_mean, bn_var, out)
         p_cols = const.tile([P, 48], F32, name="p_cols")
         var_eps = const.tile([P, 16], F32, name="var_eps")
         rstd = const.tile([P, 16], F32, name="rstd")
-        st_cols = const.tile([P, P], F32, name="st_cols")
-        s_col = st_cols[:, 0:16]
-        t_col = st_cols[:, 16:32]
+        s_col = const.tile([P, 16], F32, name="s_col")
+        t_col = const.tile([P, 16], F32, name="t_col")
         mean_s = const.tile([P, 16], F32, name="mean_s")
-        nc.gpsimd.memset(st_cols[:, 32:P], 0.0)
         warm_in = const.tile([P, 1], F32, name="warm_in")
         warm_out = const.tile([P, 1], F32, name="warm_out")
         nc.vector.memset(warm_in[:], 0.0)
@@ -109,9 +106,9 @@ def tile_modelnew_kernel(tc, x, weight, bn_gamma, bn_beta, bn_mean, bn_var, out)
             nc.gpsimd.tensor_tensor(out=rstd[:], in0=var_eps[:], in1=minus_half[:], op=ALU.pow)
 
         def scale_and_shift():
-            nc.vector.tensor_mul(s_col, p_cols[:, 0:16], rstd[:])
-            nc.vector.tensor_mul(mean_s[:], p_cols[:, 32:48], s_col)
-            nc.vector.tensor_sub(t_col, p_cols[:, 16:32], mean_s[:])
+            nc.vector.tensor_mul(s_col[:], p_cols[:, 0:16], rstd[:])
+            nc.vector.tensor_mul(mean_s[:], p_cols[:, 32:48], s_col[:])
+            nc.vector.tensor_sub(t_col[:], p_cols[:, 16:32], mean_s[:])
 
         def transpose_x(t, gg):
             xt = ps_tr.tile([P, 2, 2, P], F32, name="xt", tag="bank")
@@ -190,19 +187,22 @@ def tile_modelnew_kernel(tc, x, weight, bn_gamma, bn_beta, bn_mean, bn_var, out)
             )
             tiles["g", u, i] = g_t
 
-        def park():
-            bank = ps_tr.tile([P, P], F32, name="st_bank", tag="bank")
-            nc.tensor.transpose(bank[:], st_cols[:], ident_f[:])
-            st_rows = const.tile([32, P], F32, name="st_rows")
-            nc.scalar.copy(out=st_rows[:], in_=bank[0:32, :])
-            nc.sync.dma_start(out=out[B - 2 : B, :].rearrange("v (r c) -> (v r) c", c=P), in_=st_rows[:])
-            for name, row in (("s", B - 2), ("t", B - 1)):
-                wide = row_pool.tile([P, N - ROW_N0], F32, name="row_" + name)
-                nc.sync.dma_start(out=wide[:], in_=out[row, ROW_N0:N].partition_broadcast(P))
-                tiles[name] = wide
+        def spread(nb):
+            for name, col in (("s", s_col), ("t", t_col)):
+                bank = ps_tr.tile([P, BLOCK], F32, name="wide_bank", tag="bank")
+                for i in range(COL_TILES):
+                    c = COL_TILES * nb + i
+                    nc.tensor.transpose(bank[:, P * i : P * i + P], col[:, c : c + 1].to_broadcast([P, P]), ident_f[:])
+                tiles["bank", name, nb] = bank
+
+        def copy_spread(nb, on_scalar):
+            for name in ("s", "t"):
+                wide = row_pool.tile([P, BLOCK], F32, name="row_%s%d" % (name, nb))
+                (nc.scalar.copy if on_scalar else nc.vector.tensor_copy)(out=wide[:], in_=tiles["bank", name, nb][:])
+                tiles[name, nb] = wide
 
         def row_of(name, nb):
-            return tiles[name][:, BLOCK * nb - ROW_N0 : BLOCK * nb - ROW_N0 + BLOCK]
+            return tiles[name, nb][:]
 
         def multiply_rows(u, r):
             nb, h = divmod(u, 2)
@@ -300,17 +300,31 @@ def tile_modelnew_kernel(tc, x, weight, bn_gamma, bn_beta, bn_mean, bn_var, out)
                 inverse_std()
             if t == 5:
                 scale_and_shift()
-        park()
-        regroup_w(0, 0, 2)
-        for g in range(PASSES):
-            quantise_x(3, g)
-            if g + 1 < PASSES:
-                regroup_w(0, g + 1, 2)
-            else:
-                regroup_w(1, 0, 2)
-            quantise_w(0, g)
-            mx4(0, g)
-            mx4(1, g)
+        spread(2)
+        spread(3)
+        regroup_w(0, 0, 0)
+        quantise_x(3, 0)
+        quantise_x(3, 1)
+        quantise_w(0, 0)
+        mx4(0, 0)
+        copy_spread(2, True)
+        regroup_w(0, 1, 2)
+        quantise_x(3, 2)
+        quantise_x(3, 3)
+        copy_spread(3, True)
+        mx4(1, 0)
+        quantise_w(0, 1)
+        mx4(0, 1)
+        mx4(1, 1)
+        regroup_w(0, 2, 2)
+        regroup_w(0, 3, 2)
+        quantise_w(0, 2)
+        mx4(0, 2)
+        mx4(1, 2)
+        regroup_w(1, 0, 2)
+        quantise_w(0, 3)
+        mx4(0, 3)
+        mx4(1, 3)
         load_w(3)
         for g in range(1, PASSES):
             regroup_w(1, g, (2,2,2,2)[g])

@@ -31,7 +31,8 @@ LAST = UNITS - 1
 
 def tile_modelnew_kernel(tc, x, weight, bn_gamma, bn_beta, bn_mean, bn_var, out):
     nc = tc.nc
-    out_v = out.rearrange("(t p) n -> p t n", p=P)
+    x_v = x.rearrange("(p t) k -> p t k", t=ROW_TILES)
+    out_v = out.rearrange("(p t) n -> p t n", t=ROW_TILES)
 
     with ExitStack() as ctx:
         const = ctx.enter_context(tc.tile_pool(name="const", bufs=1))
@@ -66,7 +67,7 @@ def tile_modelnew_kernel(tc, x, weight, bn_gamma, bn_beta, bn_mean, bn_var, out)
         p_rows = const.tile([P, P], BF16, name="p_rows")
         nc.vector.memset(p_rows[64:P, :], 0.0)
         for t in range(ROW_TILES):
-            nc.sync.dma_start(out=x_raw[t][:], in_=x[P * t : P * t + P, :])
+            nc.sync.dma_start(out=x_raw[t][:], in_=x_v[:, t, :])
             if t == 0:
                 for v, vec in enumerate((bn_gamma, bn_beta, bn_mean, bn_var)):
                     nc.sync.dma_start(out=p_rows[16 * v : 16 * v + 16, :], in_=vec.rearrange("(r c) -> r c", c=P))

@@ -303,13 +303,13 @@ def tile_modelnew_kernel(tc, x, weight, bn_gamma, bn_beta, bn_mean, bn_var, out)
                 scale_and_shift()
         spread(2)
         spread(3)
-        regroup_w(0, 0, 0)
+        regroup_w(0, 0, 2)
         quantise_x(3, 0)
         quantise_x(3, 1)
         quantise_w(0, 0)
         mx4(0, 0)
         copy_spread(2, True)
-        regroup_w(0, 1, 2)
+        regroup_w(0, 1, 1)
         quantise_x(3, 2)
         quantise_x(3, 3)
         copy_spread(3, True)
@@ -383,7 +383,7 @@ def tile_modelnew_kernel(tc, x, weight, bn_gamma, bn_beta, bn_mean, bn_var, out)
         gelu_rows(4, 1)
         scale_rows(4, 2)
         scale_rows(4, 3)
-        relu_rows(4, 0, 2)
+        relu_rows(4, 0, 2, True)
         store_rows(4, 0, 2)
         shift_rows(4, 2)
         gelu_rows(4, 2)
@@ -391,35 +391,41 @@ def tile_modelnew_kernel(tc, x, weight, bn_gamma, bn_beta, bn_mean, bn_var, out)
         gelu_rows(4, 3)
         back(2)
         second(2, (1, 3))
-        relu_rows(4, 2, 4)
+        relu_rows(4, 2, 4, True)
         store_rows(4, 2, 4)
         part(5, 0, 4)
         back(3)
         second(3, (1, 3))
-        for r in range(HALF_TILES):
-            multiply_rows(6, r)
+        multiply_rows(6, 0)
+        multiply_rows(6, 1)
+        back(5)
+        multiply_rows(6, 2)
+        multiply_rows(6, 3)
         scale_rows(6, 0)
         scale_rows(6, 1)
         shift_rows(6, 0)
         gelu_rows(6, 0)
+        second_exit(5, 0, False)
         shift_rows(6, 1)
         gelu_rows(6, 1)
         scale_rows(6, 2)
+        second_exit(5, 1, True)
+        second_exit(5, 2, False)
         scale_rows(6, 3)
-        back(5)
-        second(5, (1, 3))
-        relu_rows(6, 0, 2)
-        store_rows(6, 0, 2)
+        second_exit(5, 3, True)
+        store(5, 0, COL_TILES)
         shift_rows(6, 2)
-        gelu_rows(6, 2)
-        shift_rows(6, 3)
-        gelu_rows(6, 3)
         multiply(LAST, 0)
         first_exit(LAST, 0)
-        relu_rows(6, 2, 4)
-        store_rows(6, 2, 4)
+        shift_rows(6, 3)
+        gelu_rows(6, 2)
+        gelu_rows(6, 3)
+        relu_rows(6, 0, 2)
+        store_rows(6, 0, 2)
         multiply(LAST, 1)
         first_exit(LAST, 1)
+        relu_rows(6, 2, 4)
+        store_rows(6, 2, 4)
         multiply(LAST, 2)
         first_exit(LAST, 2)
         for i in range(2):

from contextlib import ExitStack

import concourse.mybir as mybir
from concourse.masks import make_identity

FP8X4 = mybir.dt.float8_e4m3fn_x4
BF16 = mybir.dt.bfloat16
F32 = mybir.dt.float32
U32 = mybir.dt.uint32
U8 = mybir.dt.uint8
ACT = mybir.ActivationFunctionType
ALU = mybir.AluOpType

B, K, N = 1024, 2048, 2048
EPS = 1e-5
FLOPS = 2 * B * K * N

P = 128
PACK = 4
PASSES = K // (P * PACK)
ROW_TILES = B // P
PAIRS = ROW_TILES // 2
HALF_TILES = 4
HALF = HALF_TILES * P
COL_TILES = 4
BLOCK = COL_TILES * P
N_BLOCKS = N // BLOCK
UNITS = 2 * N_BLOCKS
LAST = UNITS - 1


def tile_modelnew_kernel(tc, x, weight, bn_gamma, bn_beta, bn_mean, bn_var, out):
    nc = tc.nc
    x_v = x.rearrange("(p t) k -> p t k", t=ROW_TILES)
    out_v = out.rearrange("(p t) n -> p t n", t=ROW_TILES)

    with ExitStack() as ctx:
        const = ctx.enter_context(tc.tile_pool(name="const", bufs=1))
        keep = ctx.enter_context(tc.tile_pool(name="keep", bufs=1))
        wg_pool = ctx.enter_context(tc.tile_pool(name="wg_pool", bufs=4))
        wr_pool = ctx.enter_context(tc.tile_pool(name="wr_pool", bufs=3))
        xg_pool = ctx.enter_context(tc.tile_pool(name="xg_pool", bufs=2))
        g_pool = ctx.enter_context(tc.tile_pool(name="g_pool", bufs=3 * COL_TILES))
        o_pool = ctx.enter_context(tc.tile_pool(name="o_pool", bufs=3))
        row_pool = ctx.enter_context(tc.tile_pool(name="row_pool", bufs=1))
        ps_acc = ctx.enter_context(tc.psum_pool(name="ps_acc", bufs=4))
        ps_tr = ctx.enter_context(tc.psum_pool(name="ps_tr", bufs=4))
        ctx.enter_context(tc.manual_schedule())

        x_raw = [keep.tile([P, K], BF16, name="x_raw%d" % t) for t in range(ROW_TILES)]
        w_raw = {}
        w_codes = keep.tile([P, PASSES, N], U32, name="w_codes", align_bytes=64)
        w_scales = keep.tile([P, PASSES, N], U8, name="w_scales", align_bytes=64)
        x_codes = keep.tile([P, PASSES, B], U32, name="x_codes", align_bytes=64)
        x_scales = keep.tile([P, PASSES, B], U8, name="x_scales", align_bytes=64)

        def load_w(nb, g0=0, g1=PASSES):
            if g0 == 0:
                w_raw[nb] = wr_pool.tile([P, PACK * PASSES, BLOCK], BF16, name="w_raw")
            for g in range(g0, g1):
                rows = weight[P * PACK * g : P * PACK * g + P * PACK, BLOCK * nb : BLOCK * nb + BLOCK]
                nc.sync.dma_start(
                    out=w_raw[nb][:, PACK * g : PACK * g + PACK, :],
                    in_=rows.rearrange("(q t) n -> q t n", t=PACK),
                )

        p_rows = const.tile([P, P], BF16, name="p_rows")
        nc.vector.memset(p_rows[64:P, :], 0.0)
        for t in range(ROW_TILES):
            nc.sync.dma_start(out=x_raw[t][:], in_=x_v[:, t, :])
            if t == 0:
                for v, vec in enumerate((bn_gamma, bn_beta, bn_mean, bn_var)):
                    nc.sync.dma_start(out=p_rows[16 * v : 16 * v + 16, :], in_=vec.rearrange("(r c) -> r c", c=P))
            for g in {7: (0, 1, 2, 3)}.get(t, ()):
                load_w(0, g, g + 1)
        load_w(1)
        load_w(2)

        ident_f = const.tile([P, P], F32, name="ident_f")
        make_identity(nc, ident_f[:])
        ident_b = const.tile([P, P], BF16, name="ident_b")
        make_identity(nc, ident_b[:])
        minus_half = const.tile([P, 16], F32, name="minus_half")
        nc.gpsimd.memset(minus_half[:], -0.5)

        p_cols = const.tile([P, 48], F32, name="p_cols")
        var_eps = const.tile([P, 16], F32, name="var_eps")
        rstd = const.tile([P, 16], F32, name="rstd")
        s_col = const.tile([P, 16], F32, name="s_col")
        t_col = const.tile([P, 16], F32, name="t_col")
        mean_s = const.tile([P, 16], F32, name="mean_s")
        warm_in = const.tile([P, 1], F32, name="warm_in")
        warm_out = const.tile([P, 1], F32, name="warm_out")
        nc.vector.memset(warm_in[:], 0.0)
        tiles = {}

        def load_gelu_table():
            nc.scalar.activation(out=warm_out[:], in_=warm_in[:], func=ACT.Gelu_apprx_tanh)

        def transpose_params():
            tiles["params"] = ps_tr.tile([P, P], BF16, name="params", tag="bank")
            nc.tensor.transpose(tiles["params"][:], p_rows[:], ident_b[:])

        def inverse_std():
            nc.vector.tensor_copy(out=p_cols[:], in_=tiles["params"][:, 0:48])
            nc.vector.tensor_scalar_add(var_eps[:], tiles["params"][:, 48:64], EPS)
            nc.gpsimd.tensor_tensor(out=rstd[:], in0=var_eps[:], in1=minus_half[:], op=ALU.pow)

        def scale_and_shift():
            nc.vector.tensor_mul(s_col[:], p_cols[:, 0:16], rstd[:])
            nc.vector.tensor_mul(mean_s[:], p_cols[:, 32:48], s_col[:])
            nc.vector.tensor_sub(t_col[:], p_cols[:, 16:32], mean_s[:])

        def transpose_x(t, gg):
            xt = ps_tr.tile([P, 2, 2, P], F32, name="xt", tag="bank")
            words = x_raw[t][:].bitcast(F32)
            for e in range(2):
                for u in range(2):
                    g = 2 * gg + e
                    nc.tensor.transpose(xt[:, e, u, :], words[:, 2 * P * g + u : 2 * P * g + 2 * P : 2], ident_f[:])
            tiles["xt", t, gg] = xt

        def copy_x(t, gg, on_scalar):
            pair, odd = divmod(t, 2)
            if odd == 0 and gg == 0:
                tiles["xg", pair] = xg_pool.tile([P, PASSES, 2 * P * PACK], BF16, name="xg", align_bytes=64)
            cols = tiles["xg", pair][:, 2 * gg : 2 * gg + 2, P * PACK * odd : P * PACK * odd + P * PACK]
            dst = cols.bitcast(F32).rearrange("p g (c u) -> p g c u", u=2)
            src = tiles["xt", t, gg][:].rearrange("p g u c -> p g c u")
            (nc.scalar.copy if on_scalar else nc.vector.tensor_copy)(out=dst, in_=src)

        def quantise_x(pair, g, c0=0, c1=2):
            cols = slice(2 * P * pair + P * c0, 2 * P * pair + P * c1)
            nc.vector.quantize_mx(
                out=x_codes[:, g, cols].bitcast(FP8X4),
                scales=x_scales[:, g, cols],
                in_=tiles["xg", pair][:, g, P * PACK * c0 : P * PACK * c1],
            )

        def regroup_w(nb, g, by_scalar):
            wg = wg_pool.tile([P, BLOCK, PACK], BF16, name="wg", align_bytes=64)
            split = BLOCK - P * by_scalar
            for c0, c1, engine_copy in ((0, split, nc.vector.tensor_copy), (split, BLOCK, nc.scalar.copy)):
                if c0 == c1:
                    continue
                dst = wg[:, c0:c1, :].rearrange("p (c i) t -> p c t i", i=4)
                src = w_raw[nb][:, PACK * g : PACK * g + PACK, c0:c1].rearrange("p t (c i) -> p c t i", i=4)
                engine_copy(out=dst, in_=src)
            tiles["wg", nb, g] = wg

        def quantise_w(nb, g):
            cols = slice(BLOCK * nb, BLOCK * nb + BLOCK)
            nc.vector.quantize_mx(
                out=w_codes[:, g, cols].bitcast(FP8X4),
                scales=w_scales[:, g, cols],
                in_=tiles["wg", nb, g][:].rearrange("p n t -> p (n t)"),
            )

        def mx_pass(u, i, g):
            nb, h = divmod(u, 2)
            if g == 0:
                tiles["acc", u, i] = (ps_tr if u == 1 else ps_acc).tile([P, HALF], F32, name="acc", tag="bank")
            n_cols = slice(BLOCK * nb + P * i, BLOCK * nb + P * i + P)
            b_cols = slice(HALF * h, HALF * h + HALF)
            nc.tensor.matmul_mx(
                out=tiles["acc", u, i][:],
                lhsT=w_codes[:, g, n_cols].bitcast(FP8X4),
                lhsT_scale=w_scales[:, g, n_cols],
                rhs=x_codes[:, g, b_cols].bitcast(FP8X4),
                rhs_scale=x_scales[:, g, b_cols],
                start=(g == 0),
                stop=(g == PASSES - 1),
            )

        def multiply(u, i):
            for g in range(PASSES):
                mx_pass(u, i, g)

        def first_exit(u, i):
            col = COL_TILES * (u // 2) + i
            g_t = g_pool.tile([P, HALF], F32, name="g_t")
            nc.scalar.activation(
                out=g_t[:],
                in_=tiles["acc", u, i][:],
                func=ACT.Gelu_apprx_tanh,
                bias=t_col[:, col : col + 1],
                scale=s_col[:, col : col + 1],
            )
            tiles["g", u, i] = g_t

        def spread(nb):
            for name, col in (("s", s_col), ("t", t_col)):
                bank = ps_tr.tile([P, BLOCK], F32, name="wide_bank", tag="bank")
                for i in range(COL_TILES):
                    c = COL_TILES * nb + i
                    nc.tensor.transpose(bank[:, P * i : P * i + P], col[:, c : c + 1].to_broadcast([P, P]), ident_f[:])
                tiles["bank", name, nb] = bank

        def copy_spread(nb, on_scalar):
            for name in ("s", "t"):
                wide = row_pool.tile([P, BLOCK], F32, name="row_%s%d" % (name, nb))
                (nc.scalar.copy if on_scalar else nc.vector.tensor_copy)(out=wide[:], in_=tiles["bank", name, nb][:])
                tiles[name, nb] = wide

        def row_of(name, nb):
            return tiles[name, nb][:]

        def multiply_rows(u, r):
            nb, h = divmod(u, 2)
            acc = ps_acc.tile([P, BLOCK], F32, name="acc_r", tag="bank")
            rows = slice(HALF * h + P * r, HALF * h + P * r + P)
            n_cols = slice(BLOCK * nb, BLOCK * nb + BLOCK)
            for g in range(PASSES):
                nc.tensor.matmul_mx(
                    out=acc[:],
                    lhsT=x_codes[:, g, rows].bitcast(FP8X4),
                    lhsT_scale=x_scales[:, g, rows],
                    rhs=w_codes[:, g, n_cols].bitcast(FP8X4),
                    rhs_scale=w_scales[:, g, n_cols],
                    start=(g == 0),
                    stop=(g == PASSES - 1),
                )
            tiles["acc", u, r] = acc

        def scale_rows(u, r):
            y = g_pool.tile([P, BLOCK], F32, name="g_t")
            nc.vector.tensor_tensor(out=y[:], in0=tiles["acc", u, r][:], in1=row_of("s", u // 2), op=ALU.mult)
            tiles["y", u, r] = y

        def shift_rows(u, r):
            y = tiles["y", u, r]
            nc.vector.tensor_tensor(out=y[:], in0=y[:], in1=row_of("t", u // 2), op=ALU.add)

        def gelu_rows(u, r):
            if r == 0:
                tiles["o", u] = o_pool.tile([P, HALF_TILES, BLOCK], F32, name="o_sb")
            nc.scalar.activation(out=tiles["o", u][:, r, :], in_=tiles["y", u, r][:], func=ACT.Gelu_apprx_tanh)

        def relu_rows(u, r0, r1, on_scalar=False):
            part = tiles["o", u][:, r0:r1, :]
            if on_scalar:
                nc.scalar.activation(out=part, in_=part, func=ACT.Relu)
            else:
                nc.vector.tensor_scalar(part, part, 0.0, 0.0, op0=ALU.max, op1=ALU.add)

        def store_rows(u, r0, r1):
            nb, h = divmod(u, 2)
            nc.sync.dma_start(
                out=out_v[:, HALF_TILES * h + r0 : HALF_TILES * h + r1, BLOCK * nb : BLOCK * nb + BLOCK],
                in_=tiles["o", u][:, r0:r1, :],
            )

        def turn_back(u, i):
            tb = ps_tr.tile([P, HALF_TILES, P], F32, name="tb", tag="bank")
            for tt in range(HALF_TILES):
                nc.tensor.transpose(tb[:, tt, :], tiles["g", u, i][:, P * tt : P * tt + P], ident_f[:])
            tiles["tb", u, i] = tb

        def second_exit(u, i, on_scalar):
            if i == 0:
                tiles["o", u] = o_pool.tile([P, HALF_TILES, BLOCK], F32, name="o_sb")
            dst = tiles["o", u][:, :, P * i : P * i + P]
            if not on_scalar:
                nc.vector.tensor_scalar(dst, tiles["tb", u, i][:], 0.0, 0.0, op0=ALU.max, op1=ALU.add)
            else:
                nc.scalar.activation(out=dst, in_=tiles["tb", u, i][:], func=ACT.Relu)

        def store(u, i0, i1):
            nb, h = divmod(u, 2)
            nc.sync.dma_start(
                out=out_v[:, HALF_TILES * h : HALF_TILES * h + HALF_TILES, BLOCK * nb + P * i0 : BLOCK * nb + P * i1],
                in_=tiles["o", u][:, :, P * i0 : P * i1],
            )

        load_gelu_table()

        def tx(t):
            transpose_x(t, 0)
            transpose_x(t, 1)

        def cx(t, both_scalar):
            copy_x(t, 0, both_scalar)
            copy_x(t, 1, True)

        def qx(pair):
            for g in range(PASSES):
                quantise_x(pair, g)

        def mx4(u, g):
            for i in range(COL_TILES):
                mx_pass(u, i, g)

        for t in range(ROW_TILES):
            tx(t)
            cx(t, t in (2, 4, 6))
            if t == 1:
                transpose_params()
            if t % 2 and t < 7:
                qx(t // 2)
            if t == 2:
                inverse_std()
            if t == 5:
                scale_and_shift()
        spread(2)
        spread(3)
        regroup_w(0, 0, 2)
        quantise_x(3, 0)
        quantise_x(3, 1)
        quantise_w(0, 0)
        mx4(0, 0)
        copy_spread(2, True)
        regroup_w(0, 1, 1)
        quantise_x(3, 2)
        quantise_x(3, 3)
        copy_spread(3, True)
        mx4(1, 0)
        quantise_w(0, 1)
        mx4(0, 1)
        mx4(1, 1)
        regroup_w(0, 2, 2)
        regroup_w(0, 3, 2)
        quantise_w(0, 2)
        mx4(0, 2)
        mx4(1, 2)
        regroup_w(1, 0, 2)
        quantise_w(0, 3)
        mx4(0, 3)
        mx4(1, 3)
        load_w(3)
        for g in range(1, PASSES):
            regroup_w(1, g, (2,2,2,2)[g])
            quantise_w(1, g - 1)
        regroup_w(2, 0, (0,0,1,2)[0])
        quantise_w(1, 3)
        regroup_w(2, 1, (0,0,1,2)[1])
        quantise_w(2, 0)
        for u in range(2):
            for i in range(COL_TILES):
                first_exit(u, i)

        def part(u, k0, k1):
            for k in range(k0, k1):
                multiply(u, k)
                first_exit(u, k)

        def back(f):
            for i in range(COL_TILES):
                turn_back(f, i)

        def second(f, by_scalar):
            for i in range(COL_TILES):
                second_exit(f, i, i in by_scalar)
            store(f, 0, COL_TILES)

        part(2, 0, 2)
        regroup_w(2, 2, (0,0,1,2)[2])
        quantise_w(2, 1)
        part(2, 2, 4)
        regroup_w(2, 3, (0,0,1,2)[3])
        quantise_w(2, 2)
        back(0)
        second(0, (3,))
        quantise_w(2, 3)
        regroup_w(3, 0, (2,1,1,1)[0])
        part(3, 0, 2)
        regroup_w(3, 1, (2,1,1,1)[1])
        quantise_w(3, 0)
        part(3, 2, 4)
        regroup_w(3, 2, (2,1,1,1)[2])
        quantise_w(3, 1)
        back(1)
        second(1, (1, 3))
        regroup_w(3, 3, (2,1,1,1)[3])
        quantise_w(3, 2)
        for r in range(HALF_TILES):
            multiply_rows(4, r)
        scale_rows(4, 0)
        scale_rows(4, 1)
        quantise_w(3, 3)
        shift_rows(4, 0)
        gelu_rows(4, 0)
        shift_rows(4, 1)
        gelu_rows(4, 1)
        scale_rows(4, 2)
        scale_rows(4, 3)
        relu_rows(4, 0, 2, True)
        store_rows(4, 0, 2)
        shift_rows(4, 2)
        gelu_rows(4, 2)
        shift_rows(4, 3)
        gelu_rows(4, 3)
        back(2)
        second(2, (1, 3))
        relu_rows(4, 2, 4, True)
        store_rows(4, 2, 4)
        part(5, 0, 4)
        back(3)
        second(3, (1, 3))
        multiply_rows(6, 0)
        multiply_rows(6, 1)
        back(5)
        multiply_rows(6, 2)
        multiply_rows(6, 3)
        scale_rows(6, 0)
        scale_rows(6, 1)
        shift_rows(6, 0)
        gelu_rows(6, 0)
        second_exit(5, 0, False)
        shift_rows(6, 1)
        gelu_rows(6, 1)
        scale_rows(6, 2)
        second_exit(5, 1, True)
        second_exit(5, 2, False)
        scale_rows(6, 3)
        second_exit(5, 3, True)
        store(5, 0, COL_TILES)
        shift_rows(6, 2)
        multiply(LAST, 0)
        first_exit(LAST, 0)
        shift_rows(6, 3)
        gelu_rows(6, 2)
        gelu_rows(6, 3)
        relu_rows(6, 0, 2)
        store_rows(6, 0, 2)
        multiply(LAST, 1)
        first_exit(LAST, 1)
        relu_rows(6, 2, 4)
        store_rows(6, 2, 4)
        multiply(LAST, 2)
        first_exit(LAST, 2)
        for i in range(2):
            turn_back(LAST, i)
            second_exit(LAST, i, i % 2 == 1)
        store(LAST, 0, 2)
        multiply(LAST, 3)
        first_exit(LAST, 3)
        turn_back(LAST, 2)
        second_exit(LAST, 2, False)
        store(LAST, 2, 3)
        turn_back(LAST, 3)
        second_exit(LAST, 3, True)
        store(LAST, 3, 4)
